import numpy as np
import ml_dtypes

BF16 = ml_dtypes.bfloat16


def bf(x):
    return np.asarray(x, np.float32).astype(BF16)


def f32(x):
    return np.asarray(x, np.float32)


def f64(x):
    return np.asarray(x).astype(np.float64)


def striped(idx):
    return np.tile(idx.reshape(-1, 16).T, (8, 1))


D, S, H, O, N, ONE = 128, 4096, 512, 256, 1024, 1


def setup_inputs():
    return {
        "x": bf(np.random.standard_normal((D, S))),
        "w1": bf(np.random.standard_normal((D, H)) / np.sqrt(D)),
        "b1": f32(0.5 * np.random.standard_normal((H, ONE))),
        "w2": bf(np.random.standard_normal((H, O)) / np.sqrt(H)),
        "b2": f32(0.5 * np.random.standard_normal((O, ONE))),
        "w1_p": f32(1.3 + 0.1 * np.random.standard_normal(ONE)),
        "b1_p": f32(0.7 + 0.1 * np.random.standard_normal(ONE)),
        "w2_p": f32(0.8 + 0.1 * np.random.standard_normal(ONE)),
        "b2_p": f32(1.2 + 0.1 * np.random.standard_normal(ONE)),
        "offs": striped(np.random.permutation(S)[:N]),
    }


def reference(x, w1, b1, w2, b2, w1_p, b1_p, w2_p, b2_p, offs):
    idx = offs[:16].T.reshape(-1)
    h = np.maximum(f64(w1_p) * (f64(w1).T @ f64(x)[:, idx]) + f64(b1_p) * f64(b1), 0.0)
    return f64(w2_p) * (f64(w2).T @ h) + f64(b2_p) * f64(b2)

@@ -1,0 +1,106 @@
+import concourse.mybir as mybir
+
+BF16, F32, U16 = mybir.dt.bfloat16, mybir.dt.float32, mybir.dt.uint16
+MULT, ADD = mybir.AluOpType.mult, mybir.AluOpType.add
+RELU, IDENTITY = mybir.ActivationFunctionType.Relu, mybir.ActivationFunctionType.Identity
+
+P = 128
+S = 4096
+H = 512
+O = 256
+N = 1024
+PIECE = 512
+N_PIECES = N // PIECE
+H_BLOCKS = H // P
+O_BLOCKS = O // P
+
+FLOPS = 2 * P * H * N + 2 * H * O * N
+BYTES = 2 * (P * N + P * H + H * O) + 4 * (H + O + 4) + 2 * P * (N // 16) + 4 * O * N
+
+BIAS1 = 0
+BIAS2 = BIAS1 + H_BLOCKS
+SCALE1 = BIAS2 + O_BLOCKS
+SCALE2 = SCALE1 + 1
+N_CONSTS = SCALE2 + 1
+
+
+def tile_feathernet_kernel(tc, x, w1, b1, w2, b2, w1_p, b1_p, w2_p, b2_p, offs, out):
+    nc = tc.nc
+    with (
+        tc.tile_pool(name="held", bufs=1) as held,
+        tc.tile_pool(name="work", bufs=2) as work,
+        tc.tile_pool(name="staging", bufs=4) as staging,
+        tc.psum_pool(name="psum_consts", bufs=1) as psum_consts,
+        tc.psum_pool(name="psum", bufs=7) as psum,
+    ):
+        offsets = held.tile([P, N // 16], U16, name="offsets")
+        nc.sync.dma_start(offsets[:], offs)
+        b1_row = held.tile([1, H], F32, name="b1_row")
+        nc.sync.dma_start(b1_row[:], b1.rearrange("h one -> one h"))
+        b1_scale = held.tile([1, 1], F32, name="b1_scale")
+        nc.sync.dma_start(b1_scale[:], b1_p.unsqueeze(0))
+        w1_scale = held.tile([1, 1], F32, name="w1_scale")
+        nc.sync.dma_start(w1_scale[:], w1_p.unsqueeze(0))
+        b2_row = held.tile([1, O], F32, name="b2_row")
+        nc.scalar.dma_start(b2_row[:], b2.rearrange("o one -> one o"))
+        b2_scale = held.tile([1, 1], F32, name="b2_scale")
+        nc.scalar.dma_start(b2_scale[:], b2_p.unsqueeze(0))
+        w2_scale = held.tile([1, 1], F32, name="w2_scale")
+        nc.scalar.dma_start(w2_scale[:], w2_p.unsqueeze(0))
+        x_sb = held.tile([P, S], BF16, name="x_sb")
+        nc.sync.dma_start(x_sb[:], x)
+        w1_sb = held.tile([P, H], BF16, name="w1_sb")
+        nc.scalar.dma_start(w1_sb[:], w1)
+        w2_sb = held.tile([P, H_BLOCKS, O], BF16, name="w2_sb")
+        nc.scalar.dma_start(w2_sb[:], w2.rearrange("(k p) o -> p k o", p=P))
+        ones_row = held.tile([1, P], F32, name="ones_row")
+        nc.vector.memset(ones_row[:], 1.0)
+
+        consts_ps = psum_consts.tile([P, N_CONSTS], F32, name="consts_ps")
+        for k in range(H_BLOCKS):
+            nc.tensor.matmul(
+                consts_ps[:, BIAS1 + k : BIAS1 + k + 1], b1_row[:, k * P : (k + 1) * P], b1_scale[:],
+                start=True, stop=True,
+            )
+        for c in range(O_BLOCKS):
+            nc.tensor.matmul(
+                consts_ps[:, BIAS2 + c : BIAS2 + c + 1], b2_row[:, c * P : (c + 1) * P], b2_scale[:],
+                start=True, stop=True,
+            )
+        nc.tensor.matmul(consts_ps[:, SCALE1 : SCALE1 + 1], ones_row[:], w1_scale[:], start=True, stop=True)
+        nc.tensor.matmul(consts_ps[:, SCALE2 : SCALE2 + 1], ones_row[:], w2_scale[:], start=True, stop=True)
+        consts = held.tile([P, N_CONSTS], F32, name="consts")
+        nc.vector.tensor_copy(consts[:], consts_ps[:])
+
+        h_sb = {}
+        for piece in range(N_PIECES):
+            picked = x_sb[:].indirect(offsets[:, piece * (PIECE // 16) : (piece + 1) * (PIECE // 16)])
+            for k in range(H_BLOCKS):
+                h_ps = psum.tile([P, PIECE], F32, name="h_ps", tag="bank")
+                nc.tensor.matmul(h_ps[:], w1_sb[:, k * P : (k + 1) * P], picked, start=True, stop=True)
+                h_sb[piece, k] = held.tile([P, PIECE], BF16, name=f"h_sb{piece}_{k}")
+                scale1 = consts[:, SCALE1 : SCALE1 + 1]
+                bias1 = consts[:, BIAS1 + k : BIAS1 + k + 1]
+                if k % 2 == 0:
+                    nc.scalar.activation(h_sb[piece, k][:], h_ps[:], RELU, bias=bias1, scale=scale1)
+                else:
+                    affine = work.tile([P, PIECE], BF16, name="affine")
+                    nc.vector.tensor_scalar(affine[:], h_ps[:], scale1, bias1, MULT, ADD)
+                    nc.vector.tensor_scalar_max(h_sb[piece, k][:], affine[:], 0.0)
+
+        for piece in range(N_PIECES):
+            for c in range(O_BLOCKS):
+                out_ps = psum.tile([P, PIECE], F32, name="out_ps", tag="bank")
+                for k in range(H_BLOCKS):
+                    nc.tensor.matmul(
+                        out_ps[:], w2_sb[:, k, c * P : (c + 1) * P], h_sb[piece, k][:],
+                        start=(k == 0), stop=(k == H_BLOCKS - 1),
+                    )
+                out_sb = staging.tile([P, PIECE], F32, name="out_sb")
+                scale2 = consts[:, SCALE2 : SCALE2 + 1]
+                bias2 = consts[:, BIAS2 + c : BIAS2 + c + 1]
+                if c % 2 == 0:
+                    nc.scalar.activation(out_sb[:], out_ps[:], IDENTITY, bias=bias2, scale=scale2)
+                else:
+                    nc.vector.tensor_scalar(out_sb[:], out_ps[:], scale2, bias2, MULT, ADD)
+                nc.sync.dma_start(out[c * P : (c + 1) * P, piece * PIECE : (piece + 1) * PIECE], out_sb[:])

@@ -23,6 +23,8 @@ SCALE1 = BIAS2 + O_BLOCKS
 SCALE2 = SCALE1 + 1
 N_CONSTS = SCALE2 + 1
 
+WARM_MATMULS = 7
+
 
 def tile_feathernet_kernel(tc, x, w1, b1, w2, b2, w1_p, b1_p, w2_p, b2_p, offs, out):
     nc = tc.nc
@@ -55,6 +57,12 @@ def tile_feathernet_kernel(tc, x, w1, b1, w2, b2, w1_p, b1_p, w2_p, b2_p, offs, 
         nc.scalar.dma_start(w2_sb[:], w2.rearrange("(k p) o -> p k o", p=P))
         ones_row = held.tile([1, P], F32, name="ones_row")
         nc.vector.memset(ones_row[:], 1.0)
+
+        zeros = held.tile([P, PIECE], BF16, name="zeros")
+        nc.gpsimd.memset(zeros[:], 0.0)
+        warm_ps = psum.tile([P, PIECE], F32, name="warm_ps", tag="bank")
+        for w in range(WARM_MATMULS):
+            nc.tensor.matmul(warm_ps[:], zeros[:, 0:P], zeros[:], start=True, stop=True)
 
         consts_ps = psum_consts.tile([P, N_CONSTS], F32, name="consts_ps")
         for k in range(H_BLOCKS):

@@ -13,17 +13,10 @@ PIECE = 512
 N_PIECES = N // PIECE
 H_BLOCKS = H // P
 O_BLOCKS = O // P
+PSUM_BANKS = 8
 
 FLOPS = 2 * P * H * N + 2 * H * O * N
 BYTES = 2 * (P * N + P * H + H * O) + 4 * (H + O + 4) + 2 * P * (N // 16) + 4 * O * N
-
-BIAS1 = 0
-BIAS2 = BIAS1 + H_BLOCKS
-SCALE1 = BIAS2 + O_BLOCKS
-SCALE2 = SCALE1 + 1
-N_CONSTS = SCALE2 + 1
-
-WARM_MATMULS = 7
 
 
 def tile_feathernet_kernel(tc, x, w1, b1, w2, b2, w1_p, b1_p, w2_p, b2_p, offs, out):
@@ -32,53 +25,35 @@ def tile_feathernet_kernel(tc, x, w1, b1, w2, b2, w1_p, b1_p, w2_p, b2_p, offs, 
         tc.tile_pool(name="held", bufs=1) as held,
         tc.tile_pool(name="work", bufs=2) as work,
         tc.tile_pool(name="staging", bufs=4) as staging,
-        tc.psum_pool(name="psum_consts", bufs=1) as psum_consts,
-        tc.psum_pool(name="psum", bufs=7) as psum,
+        tc.psum_pool(name="psum", bufs=PSUM_BANKS) as psum,
     ):
+        x_sb = held.tile([P, S], BF16, name="x_sb")
+        nc.scalar.dma_start(x_sb[:], x)
         offsets = held.tile([P, N // 16], U16, name="offsets")
         nc.sync.dma_start(offsets[:], offs)
-        b1_row = held.tile([1, H], F32, name="b1_row")
-        nc.sync.dma_start(b1_row[:], b1.rearrange("h one -> one h"))
-        b1_scale = held.tile([1, 1], F32, name="b1_scale")
-        nc.sync.dma_start(b1_scale[:], b1_p.unsqueeze(0))
-        w1_scale = held.tile([1, 1], F32, name="w1_scale")
-        nc.sync.dma_start(w1_scale[:], w1_p.unsqueeze(0))
-        b2_row = held.tile([1, O], F32, name="b2_row")
-        nc.scalar.dma_start(b2_row[:], b2.rearrange("o one -> one o"))
-        b2_scale = held.tile([1, 1], F32, name="b2_scale")
-        nc.scalar.dma_start(b2_scale[:], b2_p.unsqueeze(0))
-        w2_scale = held.tile([1, 1], F32, name="w2_scale")
-        nc.scalar.dma_start(w2_scale[:], w2_p.unsqueeze(0))
-        x_sb = held.tile([P, S], BF16, name="x_sb")
-        nc.sync.dma_start(x_sb[:], x)
         w1_sb = held.tile([P, H], BF16, name="w1_sb")
-        nc.scalar.dma_start(w1_sb[:], w1)
+        nc.sync.dma_start(w1_sb[:], w1)
+
+        scale1 = held.tile([P, 1], F32, name="scale1")
+        b1_scale = held.tile([P, 1], F32, name="b1_scale")
+        b1_sb = held.tile([P, H_BLOCKS], F32, name="b1_sb")
+        scale2 = held.tile([P, 1], F32, name="scale2")
+        b2_scale = held.tile([P, 1], F32, name="b2_scale")
+        b2_sb = held.tile([P, O_BLOCKS], F32, name="b2_sb")
+        with nc.allow_non_contiguous_dma(reason="small vectors, one element to a partition"):
+            nc.sync.dma_start(scale1[:], w1_p.partition_broadcast(P))
+            nc.sync.dma_start(b1_scale[:], b1_p.partition_broadcast(P))
+            nc.sync.dma_start(b1_sb[:], b1.rearrange("(k p) one -> p (k one)", p=P))
+            nc.scalar.dma_start(scale2[:], w2_p.partition_broadcast(P))
+            nc.scalar.dma_start(b2_scale[:], b2_p.partition_broadcast(P))
+            nc.scalar.dma_start(b2_sb[:], b2.rearrange("(c p) one -> p (c one)", p=P))
         w2_sb = held.tile([P, H_BLOCKS, O], BF16, name="w2_sb")
         nc.scalar.dma_start(w2_sb[:], w2.rearrange("(k p) o -> p k o", p=P))
-        ones_row = held.tile([1, P], F32, name="ones_row")
-        nc.vector.memset(ones_row[:], 1.0)
 
-        zeros = held.tile([P, PIECE], BF16, name="zeros")
-        nc.gpsimd.memset(zeros[:], 0.0)
-        warm_ps = psum.tile([P, PIECE], F32, name="warm_ps", tag="bank")
-        for w in range(WARM_MATMULS):
-            nc.tensor.matmul(warm_ps[:], zeros[:, 0:P], zeros[:], start=True, stop=True)
-
-        consts_ps = psum_consts.tile([P, N_CONSTS], F32, name="consts_ps")
-        for k in range(H_BLOCKS):
-            nc.tensor.matmul(
-                consts_ps[:, BIAS1 + k : BIAS1 + k + 1], b1_row[:, k * P : (k + 1) * P], b1_scale[:],
-                start=True, stop=True,
-            )
-        for c in range(O_BLOCKS):
-            nc.tensor.matmul(
-                consts_ps[:, BIAS2 + c : BIAS2 + c + 1], b2_row[:, c * P : (c + 1) * P], b2_scale[:],
-                start=True, stop=True,
-            )
-        nc.tensor.matmul(consts_ps[:, SCALE1 : SCALE1 + 1], ones_row[:], w1_scale[:], start=True, stop=True)
-        nc.tensor.matmul(consts_ps[:, SCALE2 : SCALE2 + 1], ones_row[:], w2_scale[:], start=True, stop=True)
-        consts = held.tile([P, N_CONSTS], F32, name="consts")
-        nc.vector.tensor_copy(consts[:], consts_ps[:])
+        bias1 = held.tile([P, H_BLOCKS], F32, name="bias1")
+        nc.vector.tensor_scalar_mul(bias1[:], b1_sb[:], b1_scale[:])
+        bias2 = held.tile([P, O_BLOCKS], F32, name="bias2")
+        nc.vector.tensor_scalar_mul(bias2[:], b2_sb[:], b2_scale[:])
 
         h_sb = {}
         for piece in range(N_PIECES):
@@ -87,13 +62,13 @@ def tile_feathernet_kernel(tc, x, w1, b1, w2, b2, w1_p, b1_p, w2_p, b2_p, offs, 
                 h_ps = psum.tile([P, PIECE], F32, name="h_ps", tag="bank")
                 nc.tensor.matmul(h_ps[:], w1_sb[:, k * P : (k + 1) * P], picked, start=True, stop=True)
                 h_sb[piece, k] = held.tile([P, PIECE], BF16, name=f"h_sb{piece}_{k}")
-                scale1 = consts[:, SCALE1 : SCALE1 + 1]
-                bias1 = consts[:, BIAS1 + k : BIAS1 + k + 1]
                 if k % 2 == 0:
-                    nc.scalar.activation(h_sb[piece, k][:], h_ps[:], RELU, bias=bias1, scale=scale1)
+                    nc.scalar.activation(
+                        h_sb[piece, k][:], h_ps[:], RELU, bias=bias1[:, k : k + 1], scale=scale1[:]
+                    )
                 else:
                     affine = work.tile([P, PIECE], BF16, name="affine")
-                    nc.vector.tensor_scalar(affine[:], h_ps[:], scale1, bias1, MULT, ADD)
+                    nc.vector.tensor_scalar(affine[:], h_ps[:], scale1[:], bias1[:, k : k + 1], MULT, ADD)
                     nc.vector.tensor_scalar_max(h_sb[piece, k][:], affine[:], 0.0)
 
         for piece in range(N_PIECES):
@@ -105,10 +80,10 @@ def tile_feathernet_kernel(tc, x, w1, b1, w2, b2, w1_p, b1_p, w2_p, b2_p, offs, 
                         start=(k == 0), stop=(k == H_BLOCKS - 1),
                     )
                 out_sb = staging.tile([P, PIECE], F32, name="out_sb")
-                scale2 = consts[:, SCALE2 : SCALE2 + 1]
-                bias2 = consts[:, BIAS2 + c : BIAS2 + c + 1]
                 if c % 2 == 0:
-                    nc.scalar.activation(out_sb[:], out_ps[:], IDENTITY, bias=bias2, scale=scale2)
+                    nc.scalar.activation(
+                        out_sb[:], out_ps[:], IDENTITY, bias=bias2[:, c : c + 1], scale=scale2[:]
+                    )
                 else:
-                    nc.vector.tensor_scalar(out_sb[:], out_ps[:], scale2, bias2, MULT, ADD)
+                    nc.vector.tensor_scalar(out_sb[:], out_ps[:], scale2[:], bias2[:, c : c + 1], MULT, ADD)
                 nc.sync.dma_start(out[c * P : (c + 1) * P, piece * PIECE : (piece + 1) * PIECE], out_sb[:])

@@ -41,14 +41,15 @@ def tile_feathernet_kernel(tc, x, w1, b1, w2, b2, w1_p, b1_p, w2_p, b2_p, offs, 
         b2_scale = held.tile([P, 1], F32, name="b2_scale")
         b2_sb = held.tile([P, O_BLOCKS], F32, name="b2_sb")
         with nc.allow_non_contiguous_dma(reason="small vectors, one element to a partition"):
-            nc.sync.dma_start(scale1[:], w1_p.partition_broadcast(P))
-            nc.sync.dma_start(b1_scale[:], b1_p.partition_broadcast(P))
-            nc.sync.dma_start(b1_sb[:], b1.rearrange("(k p) one -> p (k one)", p=P))
+            nc.scalar.dma_start(scale1[:], w1_p.partition_broadcast(P))
+            nc.scalar.dma_start(b1_scale[:], b1_p.partition_broadcast(P))
+            nc.scalar.dma_start(b1_sb[:], b1.rearrange("(k p) one -> p (k one)", p=P))
+        w2_sb = held.tile([P, H_BLOCKS, O], BF16, name="w2_sb")
+        nc.scalar.dma_start(w2_sb[:], w2.rearrange("(k p) o -> p k o", p=P))
+        with nc.allow_non_contiguous_dma(reason="small vectors, one element to a partition"):
             nc.scalar.dma_start(scale2[:], w2_p.partition_broadcast(P))
             nc.scalar.dma_start(b2_scale[:], b2_p.partition_broadcast(P))
             nc.scalar.dma_start(b2_sb[:], b2.rearrange("(c p) one -> p (c one)", p=P))
-        w2_sb = held.tile([P, H_BLOCKS, O], BF16, name="w2_sb")
-        nc.scalar.dma_start(w2_sb[:], w2.rearrange("(k p) o -> p k o", p=P))
 
         bias1 = held.tile([P, H_BLOCKS], F32, name="bias1")
         nc.vector.tensor_scalar_mul(bias1[:], b1_sb[:], b1_scale[:])

@@ -14,6 +14,7 @@ N_PIECES = N // PIECE
 H_BLOCKS = H // P
 O_BLOCKS = O // P
 PSUM_BANKS = 8
+OUT_CHUNK = 256
 
 FLOPS = 2 * P * H * N + 2 * H * O * N
 BYTES = 2 * (P * N + P * H + H * O) + 4 * (H + O + 4) + 2 * P * (N // 16) + 4 * O * N
@@ -72,19 +73,22 @@ def tile_feathernet_kernel(tc, x, w1, b1, w2, b2, w1_p, b1_p, w2_p, b2_p, offs, 
                     nc.vector.tensor_scalar(affine[:], h_ps[:], scale1[:], bias1[:, k : k + 1], MULT, ADD)
                     nc.vector.tensor_scalar_max(h_sb[piece, k][:], affine[:], 0.0)
 
-        for piece in range(N_PIECES):
+        for chunk in range(N // OUT_CHUNK):
+            piece, first = divmod(chunk * OUT_CHUNK, PIECE)
             for c in range(O_BLOCKS):
-                out_ps = psum.tile([P, PIECE], F32, name="out_ps", tag="bank")
+                out_ps = psum.tile([P, OUT_CHUNK], F32, name="out_ps", tag="bank")
                 for k in range(H_BLOCKS):
                     nc.tensor.matmul(
-                        out_ps[:], w2_sb[:, k, c * P : (c + 1) * P], h_sb[piece, k][:],
+                        out_ps[:], w2_sb[:, k, c * P : (c + 1) * P], h_sb[piece, k][:, first : first + OUT_CHUNK],
                         start=(k == 0), stop=(k == H_BLOCKS - 1),
                     )
-                out_sb = staging.tile([P, PIECE], F32, name="out_sb")
+                out_sb = staging.tile([P, OUT_CHUNK], F32, name="out_sb")
                 if c % 2 == 0:
                     nc.scalar.activation(
                         out_sb[:], out_ps[:], IDENTITY, bias=bias2[:, c : c + 1], scale=scale2[:]
                     )
                 else:
                     nc.vector.tensor_scalar(out_sb[:], out_ps[:], scale2[:], bias2[:, c : c + 1], MULT, ADD)
-                nc.sync.dma_start(out[c * P : (c + 1) * P, piece * PIECE : (piece + 1) * PIECE], out_sb[:])
+                nc.sync.dma_start(
+                    out[c * P : (c + 1) * P, chunk * OUT_CHUNK : (chunk + 1) * OUT_CHUNK], out_sb[:]
+                )

@@ -25,7 +25,7 @@ def tile_feathernet_kernel(tc, x, w1, b1, w2, b2, w1_p, b1_p, w2_p, b2_p, offs, 
     with (
         tc.tile_pool(name="held", bufs=1) as held,
         tc.tile_pool(name="work", bufs=2) as work,
-        tc.tile_pool(name="staging", bufs=4) as staging,
+        tc.tile_pool(name="staging", bufs=(N // OUT_CHUNK) * O_BLOCKS) as staging,
         tc.psum_pool(name="psum", bufs=PSUM_BANKS) as psum,
     ):
         x_sb = held.tile([P, S], BF16, name="x_sb")

@@ -32,8 +32,11 @@ def tile_feathernet_kernel(tc, x, w1, b1, w2, b2, w1_p, b1_p, w2_p, b2_p, offs, 
         nc.scalar.dma_start(x_sb[:], x)
         offsets = held.tile([P, N // 16], U16, name="offsets")
         nc.sync.dma_start(offsets[:], offs)
-        w1_sb = held.tile([P, H], BF16, name="w1_sb")
-        nc.sync.dma_start(w1_sb[:], w1)
+        w1_first = held.tile([P, P], BF16, name="w1_first")
+        nc.sync.dma_start(w1_first[:], w1[:, :P])
+        w1_rest = held.tile([P, H - P], BF16, name="w1_rest")
+        nc.scalar.dma_start(w1_rest[:], w1[:, P:])
+        w1_block = [w1_first[:]] + [w1_rest[:, (k - 1) * P : k * P] for k in range(1, H_BLOCKS)]
 
         scale1 = held.tile([P, 1], F32, name="scale1")
         b1_scale = held.tile([P, 1], F32, name="b1_scale")
@@ -62,7 +65,7 @@ def tile_feathernet_kernel(tc, x, w1, b1, w2, b2, w1_p, b1_p, w2_p, b2_p, offs, 
             picked = x_sb[:].indirect(offsets[:, piece * (PIECE // 16) : (piece + 1) * (PIECE // 16)])
             for k in range(H_BLOCKS):
                 h_ps = psum.tile([P, PIECE], F32, name="h_ps", tag="bank")
-                nc.tensor.matmul(h_ps[:], w1_sb[:, k * P : (k + 1) * P], picked, start=True, stop=True)
+                nc.tensor.matmul(h_ps[:], w1_block[k], picked, start=True, stop=True)
                 h_sb[piece, k] = held.tile([P, PIECE], BF16, name=f"h_sb{piece}_{k}")
                 if k % 2 == 0:
                     nc.scalar.activation(

@@ -14,7 +14,8 @@ N_PIECES = N // PIECE
 H_BLOCKS = H // P
 O_BLOCKS = O // P
 PSUM_BANKS = 8
-OUT_CHUNK = 256
+OUT_WIDTHS = [256, 256, 256, 128, 128]
+assert sum(OUT_WIDTHS) == N
 
 FLOPS = 2 * P * H * N + 2 * H * O * N
 BYTES = 2 * (P * N + P * H + H * O) + 4 * (H + O + 4) + 2 * P * (N // 16) + 4 * O * N
@@ -25,7 +26,7 @@ def tile_feathernet_kernel(tc, x, w1, b1, w2, b2, w1_p, b1_p, w2_p, b2_p, offs, 
     with (
         tc.tile_pool(name="held", bufs=1) as held,
         tc.tile_pool(name="work", bufs=2) as work,
-        tc.tile_pool(name="staging", bufs=(N // OUT_CHUNK) * O_BLOCKS) as staging,
+        tc.tile_pool(name="staging", bufs=len(OUT_WIDTHS) * O_BLOCKS) as staging,
         tc.psum_pool(name="psum", bufs=PSUM_BANKS) as psum,
     ):
         x_sb = held.tile([P, S], BF16, name="x_sb")
@@ -76,22 +77,24 @@ def tile_feathernet_kernel(tc, x, w1, b1, w2, b2, w1_p, b1_p, w2_p, b2_p, offs, 
                     nc.vector.tensor_scalar(affine[:], h_ps[:], scale1[:], bias1[:, k : k + 1], MULT, ADD)
                     nc.vector.tensor_scalar_max(h_sb[piece, k][:], affine[:], 0.0)
 
-        for chunk in range(N // OUT_CHUNK):
-            piece, first = divmod(chunk * OUT_CHUNK, PIECE)
+        sample = 0
+        for width in OUT_WIDTHS:
+            piece, first = divmod(sample, PIECE)
             for c in range(O_BLOCKS):
-                out_ps = psum.tile([P, OUT_CHUNK], F32, name="out_ps", tag="bank")
+                out_ps = psum.tile([P, width], F32, name="out_ps", tag="bank")
                 for k in range(H_BLOCKS):
                     nc.tensor.matmul(
-                        out_ps[:], w2_sb[:, k, c * P : (c + 1) * P], h_sb[piece, k][:, first : first + OUT_CHUNK],
+                        out_ps[:], w2_sb[:, k, c * P : (c + 1) * P], h_sb[piece, k][:, first : first + width],
                         start=(k == 0), stop=(k == H_BLOCKS - 1),
                     )
-                out_sb = staging.tile([P, OUT_CHUNK], F32, name="out_sb")
+                out_sb = staging.tile([P, 256], F32, name="out_sb")
                 if c % 2 == 0:
                     nc.scalar.activation(
-                        out_sb[:], out_ps[:], IDENTITY, bias=bias2[:, c : c + 1], scale=scale2[:]
+                        out_sb[:, :width], out_ps[:], IDENTITY, bias=bias2[:, c : c + 1], scale=scale2[:]
                     )
                 else:
-                    nc.vector.tensor_scalar(out_sb[:], out_ps[:], scale2[:], bias2[:, c : c + 1], MULT, ADD)
-                nc.sync.dma_start(
-                    out[c * P : (c + 1) * P, chunk * OUT_CHUNK : (chunk + 1) * OUT_CHUNK], out_sb[:]
-                )
+                    nc.vector.tensor_scalar(
+                        out_sb[:, :width], out_ps[:], scale2[:], bias2[:, c : c + 1], MULT, ADD
+                    )
+                nc.sync.dma_start(out[c * P : (c + 1) * P, sample : sample + width], out_sb[:, :width])
+            sample += width

@@ -14,7 +14,7 @@ N_PIECES = N // PIECE
 H_BLOCKS = H // P
 O_BLOCKS = O // P
 PSUM_BANKS = 8
-OUT_WIDTHS = [256, 256, 256, 128, 128]
+OUT_WIDTHS = [128, 128, 256, 256, 128, 128]
 assert sum(OUT_WIDTHS) == N
 
 FLOPS = 2 * P * H * N + 2 * H * O * N

@@ -30,13 +30,13 @@ def tile_feathernet_kernel(tc, x, w1, b1, w2, b2, w1_p, b1_p, w2_p, b2_p, offs, 
         tc.psum_pool(name="psum", bufs=PSUM_BANKS) as psum,
     ):
         x_sb = held.tile([P, S], BF16, name="x_sb")
-        nc.scalar.dma_start(x_sb[:], x)
+        nc.sync.dma_start(x_sb[:], x)
         offsets = held.tile([P, N // 16], U16, name="offsets")
         nc.sync.dma_start(offsets[:], offs)
         w1_first = held.tile([P, P], BF16, name="w1_first")
-        nc.sync.dma_start(w1_first[:], w1[:, :P])
+        nc.scalar.dma_start(w1_first[:], w1[:, :P])
         w1_rest = held.tile([P, H - P], BF16, name="w1_rest")
-        nc.scalar.dma_start(w1_rest[:], w1[:, P:])
+        nc.sync.dma_start(w1_rest[:], w1[:, P:])
         w1_block = [w1_first[:]] + [w1_rest[:, (k - 1) * P : k * P] for k in range(1, H_BLOCKS)]
 
         scale1 = held.tile([P, 1], F32, name="scale1")
@@ -46,15 +46,15 @@ def tile_feathernet_kernel(tc, x, w1, b1, w2, b2, w1_p, b1_p, w2_p, b2_p, offs, 
         b2_scale = held.tile([P, 1], F32, name="b2_scale")
         b2_sb = held.tile([P, O_BLOCKS], F32, name="b2_sb")
         with nc.allow_non_contiguous_dma(reason="small vectors, one element to a partition"):
-            nc.scalar.dma_start(scale1[:], w1_p.partition_broadcast(P))
-            nc.scalar.dma_start(b1_scale[:], b1_p.partition_broadcast(P))
-            nc.scalar.dma_start(b1_sb[:], b1.rearrange("(k p) one -> p (k one)", p=P))
+            nc.sync.dma_start(scale1[:], w1_p.partition_broadcast(P))
+            nc.sync.dma_start(b1_scale[:], b1_p.partition_broadcast(P))
+            nc.sync.dma_start(b1_sb[:], b1.rearrange("(k p) one -> p (k one)", p=P))
         w2_sb = held.tile([P, H_BLOCKS, O], BF16, name="w2_sb")
-        nc.scalar.dma_start(w2_sb[:], w2.rearrange("(k p) o -> p k o", p=P))
+        nc.sync.dma_start(w2_sb[:], w2.rearrange("(k p) o -> p k o", p=P))
         with nc.allow_non_contiguous_dma(reason="small vectors, one element to a partition"):
-            nc.scalar.dma_start(scale2[:], w2_p.partition_broadcast(P))
-            nc.scalar.dma_start(b2_scale[:], b2_p.partition_broadcast(P))
-            nc.scalar.dma_start(b2_sb[:], b2.rearrange("(c p) one -> p (c one)", p=P))
+            nc.sync.dma_start(scale2[:], w2_p.partition_broadcast(P))
+            nc.sync.dma_start(b2_scale[:], b2_p.partition_broadcast(P))
+            nc.sync.dma_start(b2_sb[:], b2.rearrange("(c p) one -> p (c one)", p=P))
 
         bias1 = held.tile([P, H_BLOCKS], F32, name="bias1")
         nc.vector.tensor_scalar_mul(bias1[:], b1_sb[:], b1_scale[:])

import concourse.mybir as mybir

BF16, F32, U16 = mybir.dt.bfloat16, mybir.dt.float32, mybir.dt.uint16
MULT, ADD = mybir.AluOpType.mult, mybir.AluOpType.add
RELU, IDENTITY = mybir.ActivationFunctionType.Relu, mybir.ActivationFunctionType.Identity

P = 128
S = 4096
H = 512
O = 256
N = 1024
PIECE = 512
N_PIECES = N // PIECE
H_BLOCKS = H // P
O_BLOCKS = O // P
PSUM_BANKS = 8
OUT_WIDTHS = [128, 128, 256, 256, 128, 128]
assert sum(OUT_WIDTHS) == N

FLOPS = 2 * P * H * N + 2 * H * O * N
BYTES = 2 * (P * N + P * H + H * O) + 4 * (H + O + 4) + 2 * P * (N // 16) + 4 * O * N


def tile_feathernet_kernel(tc, x, w1, b1, w2, b2, w1_p, b1_p, w2_p, b2_p, offs, out):
    nc = tc.nc
    with (
        tc.tile_pool(name="held", bufs=1) as held,
        tc.tile_pool(name="work", bufs=2) as work,
        tc.tile_pool(name="staging", bufs=len(OUT_WIDTHS) * O_BLOCKS) as staging,
        tc.psum_pool(name="psum", bufs=PSUM_BANKS) as psum,
    ):
        x_sb = held.tile([P, S], BF16, name="x_sb")
        nc.sync.dma_start(x_sb[:], x)
        offsets = held.tile([P, N // 16], U16, name="offsets")
        nc.sync.dma_start(offsets[:], offs)
        w1_first = held.tile([P, P], BF16, name="w1_first")
        nc.scalar.dma_start(w1_first[:], w1[:, :P])
        w1_rest = held.tile([P, H - P], BF16, name="w1_rest")
        nc.sync.dma_start(w1_rest[:], w1[:, P:])
        w1_block = [w1_first[:]] + [w1_rest[:, (k - 1) * P : k * P] for k in range(1, H_BLOCKS)]

        scale1 = held.tile([P, 1], F32, name="scale1")
        b1_scale = held.tile([P, 1], F32, name="b1_scale")
        b1_sb = held.tile([P, H_BLOCKS], F32, name="b1_sb")
        scale2 = held.tile([P, 1], F32, name="scale2")
        b2_scale = held.tile([P, 1], F32, name="b2_scale")
        b2_sb = held.tile([P, O_BLOCKS], F32, name="b2_sb")
        with nc.allow_non_contiguous_dma(reason="small vectors, one element to a partition"):
            nc.sync.dma_start(scale1[:], w1_p.partition_broadcast(P))
            nc.sync.dma_start(b1_scale[:], b1_p.partition_broadcast(P))
            nc.sync.dma_start(b1_sb[:], b1.rearrange("(k p) one -> p (k one)", p=P))
        w2_sb = held.tile([P, H_BLOCKS, O], BF16, name="w2_sb")
        nc.sync.dma_start(w2_sb[:], w2.rearrange("(k p) o -> p k o", p=P))
        with nc.allow_non_contiguous_dma(reason="small vectors, one element to a partition"):
            nc.sync.dma_start(scale2[:], w2_p.partition_broadcast(P))
            nc.sync.dma_start(b2_scale[:], b2_p.partition_broadcast(P))
            nc.sync.dma_start(b2_sb[:], b2.rearrange("(c p) one -> p (c one)", p=P))

        bias1 = held.tile([P, H_BLOCKS], F32, name="bias1")
        nc.vector.tensor_scalar_mul(bias1[:], b1_sb[:], b1_scale[:])
        bias2 = held.tile([P, O_BLOCKS], F32, name="bias2")
        nc.vector.tensor_scalar_mul(bias2[:], b2_sb[:], b2_scale[:])

        h_sb = {}
        for piece in range(N_PIECES):
            picked = x_sb[:].indirect(offsets[:, piece * (PIECE // 16) : (piece + 1) * (PIECE // 16)])
            for k in range(H_BLOCKS):
                h_ps = psum.tile([P, PIECE], F32, name="h_ps", tag="bank")
                nc.tensor.matmul(h_ps[:], w1_block[k], picked, start=True, stop=True)
                h_sb[piece, k] = held.tile([P, PIECE], BF16, name=f"h_sb{piece}_{k}")
                if k % 2 == 0:
                    nc.scalar.activation(
                        h_sb[piece, k][:], h_ps[:], RELU, bias=bias1[:, k : k + 1], scale=scale1[:]
                    )
                else:
                    affine = work.tile([P, PIECE], BF16, name="affine")
                    nc.vector.tensor_scalar(affine[:], h_ps[:], scale1[:], bias1[:, k : k + 1], MULT, ADD)
                    nc.vector.tensor_scalar_max(h_sb[piece, k][:], affine[:], 0.0)

        sample = 0
        for width in OUT_WIDTHS:
            piece, first = divmod(sample, PIECE)
            for c in range(O_BLOCKS):
                out_ps = psum.tile([P, width], F32, name="out_ps", tag="bank")
                for k in range(H_BLOCKS):
                    nc.tensor.matmul(
                        out_ps[:], w2_sb[:, k, c * P : (c + 1) * P], h_sb[piece, k][:, first : first + width],
                        start=(k == 0), stop=(k == H_BLOCKS - 1),
                    )
                out_sb = staging.tile([P, 256], F32, name="out_sb")
                if c % 2 == 0:
                    nc.scalar.activation(
                        out_sb[:, :width], out_ps[:], IDENTITY, bias=bias2[:, c : c + 1], scale=scale2[:]
                    )
                else:
                    nc.vector.tensor_scalar(
                        out_sb[:, :width], out_ps[:], scale2[:], bias2[:, c : c + 1], MULT, ADD
                    )
                nc.sync.dma_start(out[c * P : (c + 1) * P, sample : sample + width], out_sb[:, :width])
            sample += width
